import numpy as np
import ml_dtypes


def mxq(x, axis, fmt="e4m3"):
    dtype, down = {"e4m3": (ml_dtypes.float8_e4m3fn, 7), "e5m2": (ml_dtypes.float8_e5m2, 14)}[fmt]
    v = np.moveaxis(np.asarray(x, np.float32).astype(ml_dtypes.bfloat16).astype(np.float64), axis, -1)
    blocks = v.reshape(v.shape[:-1] + (-1, 32))
    amax = np.abs(blocks).max(-1, keepdims=True)
    byte = np.maximum(np.where(amax > 0, np.frexp(amax)[1] - 1 + 127, 0) - down, 1)
    scale = np.exp2(byte - 127.0)
    codes = (blocks / scale).astype(np.float32).astype(dtype).astype(np.float64)
    return np.moveaxis((codes * scale).reshape(v.shape), -1, axis)


WIDE = False


def mx_kscale(k):
    if not WIDE:
        return np.ones(k)
    levels = np.array([10, -10, 5, -5, 0])
    a = np.random.permutation(np.resize(levels, k // 512 * 4)).reshape(k // 512, 4)
    idx = np.arange(k)
    return np.exp2(a[idx // 512, idx % 128 // 32])


BF16 = ml_dtypes.bfloat16


def bf(x):
    return np.asarray(x, np.float32).astype(BF16)


def f64(x):
    return np.asarray(x).astype(np.float64)


B, N, D, H, DH = 1, 512, 2048, 16, 128
EPS = 1e-5


def rotate_every_two(u):
    p = u.reshape(u.shape[:-1] + (-1, 2))
    return np.stack((-p[..., 1], p[..., 0]), axis=-1).reshape(u.shape)


def apply_rotary(u, sin, cos):
    return u * cos + rotate_every_two(u) * sin


def setup_inputs():
    s = mx_kscale(D)
    r = np.exp2(-np.random.uniform(0.0, 9.0, (B, N, 1)))
    inv_freq = 1.0 / 10000.0 ** (np.arange(0, DH, 2) / DH)
    freqs = np.repeat(np.arange(N)[:, None] * inv_freq[None, :], 2, axis=-1)
    return {"x": bf((np.random.standard_normal((B, N, D)) + 0.5) * r),
            "gamma": bf((1.0 + 0.1 * np.random.standard_normal(D)) * s),
            "wq": bf(np.random.standard_normal((D, H * DH)) * 2.0 / np.sqrt(D) / s[:, None]),
            "wk": bf(np.random.standard_normal((D, DH)) / np.sqrt(D) / s[:, None]),
            "wv": bf(np.random.standard_normal((D, DH)) / np.sqrt(D) / s[:, None]),
            "sin": bf(np.sin(freqs)), "cos": bf(np.cos(freqs))}


def reference(x, gamma, wq, wk, wv, sin, cos):
    x, sin, cos = f64(x), f64(sin), f64(cos)
    mean = x.mean(-1, keepdims=True)
    var = np.square(x).mean(-1, keepdims=True) - np.square(mean)
    xn = 1.0 / np.sqrt(var + EPS) * (x - mean) * f64(gamma)
    xq = mxq(xn, 2, "e4m3")
    q = xq @ mxq(f64(wq), 0, "e4m3")
    k = xq @ mxq(f64(wk), 0, "e4m3")
    v = xq @ mxq(f64(wv), 0, "e4m3")
    q = q.reshape(B, N, H, DH).transpose(0, 2, 1, 3) * DH ** -0.5
    return apply_rotary(q, sin, cos), apply_rotary(k, sin, cos), v

@@ -1,0 +1,295 @@
+from contextlib import ExitStack
+
+import concourse.mybir as mybir
+from concourse.masks import make_identity
+
+F32 = mybir.dt.float32
+BF16 = mybir.dt.bfloat16
+U32 = mybir.dt.uint32
+U8 = mybir.dt.uint8
+FP8X4 = mybir.dt.float8_e4m3fn_x4
+ALU = mybir.AluOpType
+ACT = mybir.ActivationFunctionType
+
+P = 128
+PACK = 4
+K_PASS = P * PACK
+TOKENS = 512
+D_MODEL = 2048
+HEADS = 16
+D_HEAD = 128
+EPS = 1e-5
+
+TOKEN_TILES = TOKENS // P
+PASSES = D_MODEL // K_PASS
+ROW_GROUPS = D_MODEL // P
+PAIRS = D_HEAD // 2
+BANK = 512
+Q_CHUNKS = HEADS * D_HEAD // BANK
+HEADS_PER_CHUNK = BANK // D_HEAD
+KV = Q_CHUNKS
+CHUNKS = Q_CHUNKS + 1
+KV_WIDTH = 2 * D_HEAD
+AHEAD = 2
+RUN = 4
+BN_FIELDS = 6
+
+FLOPS = 2 * TOKENS * D_MODEL * (HEADS * D_HEAD + KV_WIDTH)
+
+
+def tile_attention_pa_kernel(tc, x, gamma, wq, wk, wv, sin, cos, out_0, out_1, out_2):
+    nc = tc.nc
+    with ExitStack() as ctx:
+        keep = ctx.enter_context(tc.tile_pool(name="keep", bufs=1))
+        small = ctx.enter_context(tc.tile_pool(name="small", bufs=4))
+        rows = ctx.enter_context(tc.tile_pool(name="rows", bufs=2))
+        loaded = ctx.enter_context(tc.tile_pool(name="loaded", bufs=AHEAD * PASSES))
+        regrouped = ctx.enter_context(tc.tile_pool(name="regrouped", bufs=AHEAD * PASSES + 2))
+        rotary = ctx.enter_context(tc.tile_pool(name="rotary", bufs=3))
+        psum = ctx.enter_context(tc.psum_pool(name="psum", bufs=8))
+        ctx.enter_context(tc.manual_schedule())
+
+        x_tiles = x.rearrange("b (t p) k -> (b t) p k", p=P)
+        x_raw = {}
+
+        def load_x(t):
+            x_raw[t] = keep.tile([P, D_MODEL], BF16, name="x_raw%d" % t)
+            nc.sync.dma_start(out=x_raw[t][:], in_=x_tiles[t])
+
+        wq_passes = wq.rearrange("(c j p) n -> c p j n", j=PACK, p=P)
+        wq_raw = {}
+
+        def load_wq(ch, c):
+            wq_raw[(ch, c)] = loaded.tile([P, PACK, BANK], BF16, name="wq_raw")
+            nc.sync.dma_start(out=wq_raw[(ch, c)][:], in_=wq_passes[c][:, :, ch * BANK : (ch + 1) * BANK])
+
+        load_x(0)
+        load_x(1)
+        load_wq(0, 0)
+        load_wq(0, 1)
+        load_x(2)
+        load_x(3)
+        load_wq(0, 2)
+        load_wq(0, 3)
+        for c in range(PASSES):
+            load_wq(1, c)
+
+        gamma_rows = keep.tile([P, P], BF16)
+        nc.vector.memset(gamma_rows[:], 0.0)
+        nc.scalar.dma_start(out=gamma_rows[0:ROW_GROUPS, :], in_=gamma.rearrange("(g p) -> g p", p=P))
+        cos_raw = keep.tile([P, TOKEN_TILES, D_HEAD], BF16)
+        nc.scalar.dma_start(out=cos_raw[:], in_=cos.rearrange("(t p) d -> p t d", p=P))
+        sin_raw = keep.tile([P, TOKEN_TILES, D_HEAD], BF16)
+        nc.scalar.dma_start(out=sin_raw[:], in_=sin.rearrange("(t p) d -> p t d", p=P))
+
+        kv_raw = keep.tile([P, ROW_GROUPS, 2, D_HEAD], BF16)
+
+        ident_f32 = keep.tile([P, P], F32)
+        make_identity(nc, ident_f32[:])
+        ident_bf16 = keep.tile([P, P], BF16)
+        make_identity(nc, ident_bf16[:])
+        one = keep.tile([P, 1], F32)
+        nc.vector.memset(one[:], 1.0)
+        table_warm = keep.tile([P, 1], F32)
+        nc.scalar.activation(out=table_warm[:], in_=one[:], func=ACT.Sqrt)
+
+        gamma_ps = psum.tile([P, P], BF16, tag="bank")
+        nc.tensor.transpose(gamma_ps[:], gamma_rows[:], ident_bf16[:])
+        gamma_col = keep.tile([P, ROW_GROUPS], F32)
+        nc.scalar.copy(out=gamma_col[:], in_=gamma_ps[:, 0:ROW_GROUPS])
+
+        def rotary_tables(scale, label):
+            by_even = keep.tile([P, TOKEN_TILES, 2, PAIRS], F32, name="by_even_" + label)
+            by_odd = keep.tile([P, TOKEN_TILES, 2, PAIRS], F32, name="by_odd_" + label)
+            cos_pairs = cos_raw[:].rearrange("p t (i e) -> p t i e", e=2)
+            sin_pairs = sin_raw[:].rearrange("p t (i e) -> p t i e", e=2)
+            for table, r, source, factor in (
+                (by_even, 0, cos_pairs[:, :, :, 0], scale),
+                (by_even, 1, sin_pairs[:, :, :, 1], scale),
+                (by_odd, 0, sin_pairs[:, :, :, 0], -scale),
+                (by_odd, 1, cos_pairs[:, :, :, 1], scale),
+            ):
+                nc.gpsimd.tensor_scalar(
+                    out=table[:, :, r, :], in0=source, scalar1=factor, scalar2=0.0, op0=ALU.mult, op1=ALU.add
+                )
+            return by_even, by_odd
+
+        q_by_even, q_by_odd = rotary_tables(D_HEAD**-0.5, "q")
+        k_by_even, k_by_odd = rotary_tables(1.0, "k")
+
+        x_codes = keep.tile([P, TOKEN_TILES, PASSES, P], U32, align_bytes=64)
+        x_scales = keep.tile([P, TOKEN_TILES, PASSES, P], U8, align_bytes=64)
+        widths = [BANK] * Q_CHUNKS + [KV_WIDTH]
+        w_codes = [
+            keep.tile([P, PASSES, widths[ch]], U32, align_bytes=64, name="w_codes%d" % ch) for ch in range(CHUNKS)
+        ]
+        w_scales = [
+            keep.tile([P, PASSES, widths[ch]], U8, align_bytes=64, name="w_scales%d" % ch) for ch in range(CHUNKS)
+        ]
+
+        def statistics(t):
+            stats = small.tile([P, PASSES, BN_FIELDS], F32)
+            for c in range(PASSES):
+                nc.vector.bn_stats(out=stats[:, c, :], in_=x_raw[t][:, c * K_PASS : (c + 1) * K_PASS])
+            mean_var = small.tile([P, 2], F32)
+            nc.vector.bn_aggr(out=mean_var[:], in_=stats[:].rearrange("p c s -> p (c s)"))
+            minus_mean = small.tile([P, 1], F32)
+            nc.vector.tensor_scalar(out=minus_mean[:], in0=mean_var[:, 0:1], scalar1=-1.0, scalar2=None, op0=ALU.mult)
+            var_eps = small.tile([P, 1], F32)
+            nc.vector.tensor_scalar(out=var_eps[:], in0=mean_var[:, 1:2], scalar1=EPS, scalar2=None, op0=ALU.add)
+            std = small.tile([P, 1], F32)
+            nc.scalar.activation(out=std[:], in_=var_eps[:], func=ACT.Sqrt)
+            return minus_mean, std
+
+        def normalise_and_transpose(t, minus_mean, std):
+            rstd = small.tile([P, 1], F32)
+            nc.vector.reciprocal(out=rstd[:], in_=std[:])
+            centred = rows.tile([P, D_MODEL], F32)
+            banks = []
+            for c in range(PASSES):
+                features = slice(c * K_PASS, (c + 1) * K_PASS)
+                nc.gpsimd.tensor_scalar(
+                    out=centred[:, features],
+                    in0=x_raw[t][:, features],
+                    scalar1=minus_mean[:, 0:1],
+                    scalar2=rstd[:, 0:1],
+                    op0=ALU.add,
+                    op1=ALU.mult,
+                )
+                flipped = psum.tile([P, PACK, P], F32, tag="bank", name="flipped")
+                for j in range(PACK):
+                    g = c * PACK + j
+                    nc.tensor.transpose(flipped[:, j, :], centred[:, g * P : (g + 1) * P], ident_f32[:])
+                banks.append(flipped)
+            return banks
+
+        def scale_and_quantise(t, banks):
+            xn = rows.tile([P, PASSES, P, PACK], BF16, align_bytes=64)
+            for c in range(PASSES):
+                nc.vector.tensor_tensor(
+                    out=xn[:, c, :, :],
+                    in0=banks[c][:].rearrange("p j m -> p m j"),
+                    in1=gamma_col[:, c * PACK : (c + 1) * PACK].unsqueeze(1).to_broadcast([P, P, PACK]),
+                    op=ALU.mult,
+                )
+            nc.vector.quantize_mx(
+                out=x_codes[:, t].rearrange("p c m -> p (c m)").bitcast(FP8X4),
+                scales=x_scales[:, t].rearrange("p c m -> p (c m)"),
+                in_=xn[:].rearrange("p c m j -> p (c m j)"),
+            )
+
+        def weight_rows(ch, c):
+            if ch == KV:
+                return kv_raw[:, c * PACK : (c + 1) * PACK, :, :].rearrange("p j s n -> p j (s n)")
+            return wq_raw[(ch, c)][:]
+
+        def regroup(ch, c):
+            grouped = regrouped.tile([P, widths[ch], PACK], BF16, tag="grouped", align_bytes=64)
+            nc.scalar.copy(
+                out=grouped[:].rearrange("p (a i) j -> p a j i", i=RUN),
+                in_=weight_rows(ch, c).rearrange("p j (a i) -> p a j i", i=RUN),
+            )
+            return grouped
+
+        def quantise(ch, c, grouped):
+            nc.vector.quantize_mx(
+                out=w_codes[ch][:, c, :].bitcast(FP8X4),
+                scales=w_scales[ch][:, c, :],
+                in_=grouped[:].rearrange("p n j -> p (n j)"),
+            )
+
+        def project(ch, t, sums):
+            for c in range(PASSES):
+                nc.tensor.matmul_mx(
+                    out=sums,
+                    lhsT=x_codes[:, t, c, :].bitcast(FP8X4),
+                    lhsT_scale=x_scales[:, t, c, :],
+                    rhs=w_codes[ch][:, c, :].bitcast(FP8X4),
+                    rhs_scale=w_scales[ch][:, c, :],
+                    start=(c == 0),
+                    stop=(c == PASSES - 1),
+                )
+
+        def rotate(result, sums, by_even, by_odd, n):
+            pairs = sums.rearrange("p n (i e) -> p e n i", e=2)
+            from_even = rotary.tile([P, 2, n, PAIRS], F32, tag="from_even")
+            nc.vector.tensor_tensor(
+                out=from_even[:], in0=pairs[:, 0:1].to_broadcast([P, 2, n, PAIRS]), in1=by_even, op=ALU.mult
+            )
+            from_odd = rotary.tile([P, 2, n, PAIRS], F32, tag="from_odd")
+            nc.vector.tensor_tensor(
+                out=from_odd[:], in0=pairs[:, 1:2].to_broadcast([P, 2, n, PAIRS]), in1=by_odd, op=ALU.mult
+            )
+            nc.gpsimd.tensor_tensor(
+                out=result.rearrange("p n (i r) -> p n i r", r=2),
+                in0=from_even[:].rearrange("p r n i -> p n i r"),
+                in1=from_odd[:].rearrange("p r n i -> p n i r"),
+                op=ALU.add,
+            )
+
+        def finish_q(ch, t, sums):
+            q_rot = rotary.tile([P, HEADS_PER_CHUNK, D_HEAD], F32, tag="rotated")
+            shape = [P, 2, HEADS_PER_CHUNK, PAIRS]
+            rotate(
+                q_rot[:],
+                sums[:].rearrange("p (n d) -> p n d", d=D_HEAD),
+                q_by_even[:, t].unsqueeze(2).to_broadcast(shape),
+                q_by_odd[:, t].unsqueeze(2).to_broadcast(shape),
+                HEADS_PER_CHUNK,
+            )
+            heads = out_0[0, ch * HEADS_PER_CHUNK : (ch + 1) * HEADS_PER_CHUNK, t * P : (t + 1) * P, :]
+            nc.sync.dma_start(out=heads.rearrange("h m d -> m h d"), in_=q_rot[:])
+
+        def finish_kv(first, sums):
+            k_rot = rotary.tile([P, 2, D_HEAD], F32, tag="rotated")
+            rotate(
+                k_rot[:],
+                sums[:, :, 0:D_HEAD],
+                k_by_even[:, first : first + 2].rearrange("p u r i -> p r u i"),
+                k_by_odd[:, first : first + 2].rearrange("p u r i -> p r u i"),
+                2,
+            )
+            v_copy = rotary.tile([P, 2, D_HEAD], F32, tag="v_copy")
+            nc.scalar.copy(out=v_copy[:], in_=sums[:, :, D_HEAD:KV_WIDTH])
+            token_rows = slice(first * P, (first + 2) * P)
+            nc.sync.dma_start(out=out_1[0, token_rows, :].rearrange("(u m) d -> m u d", u=2), in_=k_rot[:])
+            nc.sync.dma_start(out=out_2[0, token_rows, :].rearrange("(u m) d -> m u d", u=2), in_=v_copy[:])
+
+        grouped = {}
+        moments = {}
+        flipped_banks = {}
+        for s in range(TOKEN_TILES + 2):
+            if s < TOKEN_TILES:
+                moments[s] = statistics(s)
+                for ch, c in [divmod(AHEAD * s + i, PASSES) for i in range(AHEAD)]:
+                    grouped[(ch, c)] = regroup(ch, c)
+                    load_wq(ch + AHEAD, c)
+            if 0 <= s - 1 < TOKEN_TILES:
+                flipped_banks[s - 1] = normalise_and_transpose(s - 1, moments[s - 1][0], moments[s - 1][1])
+            if 0 <= s - 2:
+                scale_and_quantise(s - 2, flipped_banks[s - 2])
+        nc.sync.dma_start(out=kv_raw[:, :, 0, :], in_=wk.rearrange("(g p) n -> p g n", p=P))
+        nc.sync.dma_start(out=kv_raw[:, :, 1, :], in_=wv.rearrange("(g p) n -> p g n", p=P))
+
+        sums = {}
+        for ch in range(CHUNKS + 1):
+            if ch < CHUNKS:
+                for c in range(PASSES):
+                    quantise(ch, c, grouped[(ch, c)])
+                    if ch + AHEAD < CHUNKS:
+                        grouped[(ch + AHEAD, c)] = regroup(ch + AHEAD, c)
+            if ch < Q_CHUNKS:
+                for t in range(TOKEN_TILES):
+                    sums[(ch, t)] = psum.tile([P, BANK], F32, tag="bank", name="q_sums")
+                    project(ch, t, sums[(ch, t)][:])
+            if ch == KV:
+                for first in range(0, TOKEN_TILES, 2):
+                    sums[(ch, first)] = psum.tile([P, 2, KV_WIDTH], F32, tag="bank", name="kv_sums")
+                    for u in range(2):
+                        project(ch, first + u, sums[(ch, first)][:, u, :])
+            if 1 <= ch <= Q_CHUNKS:
+                for t in range(TOKEN_TILES):
+                    finish_q(ch - 1, t, sums[(ch - 1, t)])
+            if ch == CHUNKS:
+                for first in range(0, TOKEN_TILES, 2):
+                    finish_kv(first, sums[(KV, first)])

@@ -10,6 +10,7 @@ U8 = mybir.dt.uint8
 FP8X4 = mybir.dt.float8_e4m3fn_x4
 ALU = mybir.AluOpType
 ACT = mybir.ActivationFunctionType
+AXIS = mybir.AxisListType
 
 P = 128
 PACK = 4
@@ -30,9 +31,12 @@ HEADS_PER_CHUNK = BANK // D_HEAD
 KV = Q_CHUNKS
 CHUNKS = Q_CHUNKS + 1
 KV_WIDTH = 2 * D_HEAD
-AHEAD = 2
+AHEAD = 1
+REGROUPED = 2
+LOADED = 3
 RUN = 4
-BN_FIELDS = 6
+VECTOR_EVERY = 8
+NORM_PASSES = 2
 
 FLOPS = 2 * TOKENS * D_MODEL * (HEADS * D_HEAD + KV_WIDTH)
 
@@ -43,9 +47,9 @@ def tile_attention_pa_kernel(tc, x, gamma, wq, wk, wv, sin, cos, out_0, out_1, o
         keep = ctx.enter_context(tc.tile_pool(name="keep", bufs=1))
         small = ctx.enter_context(tc.tile_pool(name="small", bufs=4))
         rows = ctx.enter_context(tc.tile_pool(name="rows", bufs=2))
-        loaded = ctx.enter_context(tc.tile_pool(name="loaded", bufs=AHEAD * PASSES))
-        regrouped = ctx.enter_context(tc.tile_pool(name="regrouped", bufs=AHEAD * PASSES + 2))
-        rotary = ctx.enter_context(tc.tile_pool(name="rotary", bufs=3))
+        loaded = ctx.enter_context(tc.tile_pool(name="loaded", bufs=LOADED * PASSES))
+        regrouped = ctx.enter_context(tc.tile_pool(name="regrouped", bufs=REGROUPED * PASSES))
+        rotary = ctx.enter_context(tc.tile_pool(name="rotary", bufs=4))
         psum = ctx.enter_context(tc.psum_pool(name="psum", bufs=8))
         ctx.enter_context(tc.manual_schedule())
 
@@ -63,24 +67,20 @@ def tile_attention_pa_kernel(tc, x, gamma, wq, wk, wv, sin, cos, out_0, out_1, o
             wq_raw[(ch, c)] = loaded.tile([P, PACK, BANK], BF16, name="wq_raw")
             nc.sync.dma_start(out=wq_raw[(ch, c)][:], in_=wq_passes[c][:, :, ch * BANK : (ch + 1) * BANK])
 
-        load_x(0)
-        load_x(1)
-        load_wq(0, 0)
-        load_wq(0, 1)
-        load_x(2)
-        load_x(3)
-        load_wq(0, 2)
-        load_wq(0, 3)
-        for c in range(PASSES):
-            load_wq(1, c)
-
         gamma_rows = keep.tile([P, P], BF16)
         nc.vector.memset(gamma_rows[:], 0.0)
         nc.scalar.dma_start(out=gamma_rows[0:ROW_GROUPS, :], in_=gamma.rearrange("(g p) -> g p", p=P))
+        for t in range(TOKEN_TILES):
+            load_x(t)
+        for c in range(PASSES):
+            load_wq(0, c)
         cos_raw = keep.tile([P, TOKEN_TILES, D_HEAD], BF16)
-        nc.scalar.dma_start(out=cos_raw[:], in_=cos.rearrange("(t p) d -> p t d", p=P))
+        nc.sync.dma_start(out=cos_raw[:], in_=cos.rearrange("(t p) d -> p t d", p=P))
         sin_raw = keep.tile([P, TOKEN_TILES, D_HEAD], BF16)
-        nc.scalar.dma_start(out=sin_raw[:], in_=sin.rearrange("(t p) d -> p t d", p=P))
+        nc.sync.dma_start(out=sin_raw[:], in_=sin.rearrange("(t p) d -> p t d", p=P))
+        for ch in range(1, LOADED):
+            for c in range(PASSES):
+                load_wq(ch, c)
 
         kv_raw = keep.tile([P, ROW_GROUPS, 2, D_HEAD], BF16)
 
@@ -92,11 +92,10 @@ def tile_attention_pa_kernel(tc, x, gamma, wq, wk, wv, sin, cos, out_0, out_1, o
         nc.vector.memset(one[:], 1.0)
         table_warm = keep.tile([P, 1], F32)
         nc.scalar.activation(out=table_warm[:], in_=one[:], func=ACT.Sqrt)
-
-        gamma_ps = psum.tile([P, P], BF16, tag="bank")
-        nc.tensor.transpose(gamma_ps[:], gamma_rows[:], ident_bf16[:])
-        gamma_col = keep.tile([P, ROW_GROUPS], F32)
-        nc.scalar.copy(out=gamma_col[:], in_=gamma_ps[:, 0:ROW_GROUPS])
+        mean_weights = keep.tile([P, P], BF16)
+        nc.vector.tensor_scalar(
+            out=mean_weights[:], in0=ident_bf16[:], scalar1=1.0 / D_MODEL, scalar2=None, op0=ALU.mult
+        )
 
         def rotary_tables(scale, label):
             by_even = keep.tile([P, TOKEN_TILES, 2, PAIRS], F32, name="by_even_" + label)
@@ -114,9 +113,6 @@ def tile_attention_pa_kernel(tc, x, gamma, wq, wk, wv, sin, cos, out_0, out_1, o
                 )
             return by_even, by_odd
 
-        q_by_even, q_by_odd = rotary_tables(D_HEAD**-0.5, "q")
-        k_by_even, k_by_odd = rotary_tables(1.0, "k")
-
         x_codes = keep.tile([P, TOKEN_TILES, PASSES, P], U32, align_bytes=64)
         x_scales = keep.tile([P, TOKEN_TILES, PASSES, P], U8, align_bytes=64)
         widths = [BANK] * Q_CHUNKS + [KV_WIDTH]
@@ -127,18 +123,34 @@ def tile_attention_pa_kernel(tc, x, gamma, wq, wk, wv, sin, cos, out_0, out_1, o
             keep.tile([P, PASSES, widths[ch]], U8, align_bytes=64, name="w_scales%d" % ch) for ch in range(CHUNKS)
         ]
 
-        def statistics(t):
-            stats = small.tile([P, PASSES, BN_FIELDS], F32)
-            for c in range(PASSES):
-                nc.vector.bn_stats(out=stats[:, c, :], in_=x_raw[t][:, c * K_PASS : (c + 1) * K_PASS])
-            mean_var = small.tile([P, 2], F32)
-            nc.vector.bn_aggr(out=mean_var[:], in_=stats[:].rearrange("p c s -> p (c s)"))
+        def fold(t):
+            folded = psum.tile([P, P], F32, tag="bank")
+            for g in range(ROW_GROUPS):
+                nc.tensor.matmul(
+                    folded[:],
+                    lhsT=mean_weights[:],
+                    rhs=x_raw[t][:, g * P : (g + 1) * P],
+                    start=(g == 0),
+                    stop=(g == ROW_GROUPS - 1),
+                )
+            return folded
+
+        def moments(t, folded):
+            squares = keep.tile([P, D_MODEL], BF16, name="squares")
+            sum_sq = small.tile([P, 1], F32)
+            nc.scalar.activation(out=squares[:], in_=x_raw[t][:], func=ACT.Square, accum_out=sum_sq[:])
+            mean = small.tile([P, 1], F32)
+            nc.vector.tensor_reduce(out=mean[:], in_=folded[:], axis=AXIS.X, op=ALU.add)
             minus_mean = small.tile([P, 1], F32)
-            nc.vector.tensor_scalar(out=minus_mean[:], in0=mean_var[:, 0:1], scalar1=-1.0, scalar2=None, op0=ALU.mult)
-            var_eps = small.tile([P, 1], F32)
-            nc.vector.tensor_scalar(out=var_eps[:], in0=mean_var[:, 1:2], scalar1=EPS, scalar2=None, op0=ALU.add)
+            nc.vector.tensor_scalar(out=minus_mean[:], in0=mean[:], scalar1=-1.0, scalar2=None, op0=ALU.mult)
+            shift = small.tile([P, 1], F32)
+            nc.vector.tensor_scalar(
+                out=shift[:], in0=mean[:], scalar1=minus_mean[:, 0:1], scalar2=EPS, op0=ALU.mult, op1=ALU.add
+            )
             std = small.tile([P, 1], F32)
-            nc.scalar.activation(out=std[:], in_=var_eps[:], func=ACT.Sqrt)
+            nc.scalar.activation(
+                out=std[:], in_=sum_sq[:], func=ACT.Sqrt, bias=shift[:, 0:1], scale=1.0 / D_MODEL
+            )
             return minus_mean, std
 
         def normalise_and_transpose(t, minus_mean, std):
@@ -147,15 +159,16 @@ def tile_attention_pa_kernel(tc, x, gamma, wq, wk, wv, sin, cos, out_0, out_1, o
             centred = rows.tile([P, D_MODEL], F32)
             banks = []
             for c in range(PASSES):
-                features = slice(c * K_PASS, (c + 1) * K_PASS)
-                nc.gpsimd.tensor_scalar(
-                    out=centred[:, features],
-                    in0=x_raw[t][:, features],
-                    scalar1=minus_mean[:, 0:1],
-                    scalar2=rstd[:, 0:1],
-                    op0=ALU.add,
-                    op1=ALU.mult,
-                )
+                if c % NORM_PASSES == 0:
+                    features = slice(c * K_PASS, (c + NORM_PASSES) * K_PASS)
+                    nc.gpsimd.tensor_scalar(
+                        out=centred[:, features],
+                        in0=x_raw[t][:, features],
+                        scalar1=minus_mean[:, 0:1],
+                        scalar2=rstd[:, 0:1],
+                        op0=ALU.add,
+                        op1=ALU.mult,
+                    )
                 flipped = psum.tile([P, PACK, P], F32, tag="bank", name="flipped")
                 for j in range(PACK):
                     g = c * PACK + j
@@ -185,10 +198,12 @@ def tile_attention_pa_kernel(tc, x, gamma, wq, wk, wv, sin, cos, out_0, out_1, o
 
         def regroup(ch, c):
             grouped = regrouped.tile([P, widths[ch], PACK], BF16, tag="grouped", align_bytes=64)
-            nc.scalar.copy(
-                out=grouped[:].rearrange("p (a i) j -> p a j i", i=RUN),
-                in_=weight_rows(ch, c).rearrange("p j (a i) -> p a j i", i=RUN),
-            )
+            target = grouped[:].rearrange("p (a i) j -> p a j i", i=RUN)
+            source = weight_rows(ch, c).rearrange("p j (a i) -> p a j i", i=RUN)
+            if (ch * PASSES + c) % VECTOR_EVERY == VECTOR_EVERY - 1:
+                nc.vector.tensor_copy(out=target, in_=source)
+            else:
+                nc.scalar.copy(out=target, in_=source)
             return grouped
 
         def quantise(ch, c, grouped):
@@ -198,10 +213,10 @@ def tile_attention_pa_kernel(tc, x, gamma, wq, wk, wv, sin, cos, out_0, out_1, o
                 in_=grouped[:].rearrange("p n j -> p (n j)"),
             )
 
-        def project(ch, t, sums):
-            for c in range(PASSES):
+        def project(ch, c, sums):
+            for t in range(TOKEN_TILES):
                 nc.tensor.matmul_mx(
-                    out=sums,
+                    out=sums[t][:],
                     lhsT=x_codes[:, t, c, :].bitcast(FP8X4),
                     lhsT_scale=x_scales[:, t, c, :],
                     rhs=w_codes[ch][:, c, :].bitcast(FP8X4),
@@ -240,56 +255,66 @@ def tile_attention_pa_kernel(tc, x, gamma, wq, wk, wv, sin, cos, out_0, out_1, o
             heads = out_0[0, ch * HEADS_PER_CHUNK : (ch + 1) * HEADS_PER_CHUNK, t * P : (t + 1) * P, :]
             nc.sync.dma_start(out=heads.rearrange("h m d -> m h d"), in_=q_rot[:])
 
-        def finish_kv(first, sums):
-            k_rot = rotary.tile([P, 2, D_HEAD], F32, tag="rotated")
+        def finish_kv(t, sums):
+            k_rot = rotary.tile([P, 1, D_HEAD], F32, tag="k_rot")
             rotate(
                 k_rot[:],
-                sums[:, :, 0:D_HEAD],
-                k_by_even[:, first : first + 2].rearrange("p u r i -> p r u i"),
-                k_by_odd[:, first : first + 2].rearrange("p u r i -> p r u i"),
-                2,
+                sums[:, 0:D_HEAD].unsqueeze(1),
+                k_by_even[:, t].unsqueeze(2),
+                k_by_odd[:, t].unsqueeze(2),
+                1,
             )
-            v_copy = rotary.tile([P, 2, D_HEAD], F32, tag="v_copy")
-            nc.scalar.copy(out=v_copy[:], in_=sums[:, :, D_HEAD:KV_WIDTH])
-            token_rows = slice(first * P, (first + 2) * P)
-            nc.sync.dma_start(out=out_1[0, token_rows, :].rearrange("(u m) d -> m u d", u=2), in_=k_rot[:])
-            nc.sync.dma_start(out=out_2[0, token_rows, :].rearrange("(u m) d -> m u d", u=2), in_=v_copy[:])
+            v_copy = rotary.tile([P, D_HEAD], F32, tag="v_copy")
+            nc.scalar.copy(out=v_copy[:], in_=sums[:, D_HEAD:KV_WIDTH])
+            token_rows = slice(t * P, (t + 1) * P)
+            nc.sync.dma_start(out=out_1[0, token_rows, :], in_=k_rot[:, 0, :])
+            nc.sync.dma_start(out=out_2[0, token_rows, :], in_=v_copy[:])
+
+        folds = {0: fold(0)}
+        gamma_ps = psum.tile([P, P], BF16, tag="bank")
+        nc.tensor.transpose(gamma_ps[:], gamma_rows[:], ident_bf16[:])
+        gamma_col = keep.tile([P, ROW_GROUPS], F32)
+        nc.vector.tensor_copy(out=gamma_col[:], in_=gamma_ps[:, 0:ROW_GROUPS])
+        for t in range(1, TOKEN_TILES):
+            folds[t] = fold(t)
+        stats = {0: moments(0, folds[0])}
+        flipped_banks = {}
+        for s in range(TOKEN_TILES + 1):
+            if s < TOKEN_TILES:
+                flipped_banks[s] = normalise_and_transpose(s, stats[s][0], stats[s][1])
+            if s + 1 < TOKEN_TILES:
+                stats[s + 1] = moments(s + 1, folds[s + 1])
+            if s >= 1:
+                scale_and_quantise(s - 1, flipped_banks[s - 1])
+        q_by_even, q_by_odd = rotary_tables(D_HEAD**-0.5, "q")
+        k_by_even, k_by_odd = rotary_tables(1.0, "k")
 
         grouped = {}
-        moments = {}
-        flipped_banks = {}
-        for s in range(TOKEN_TILES + 2):
-            if s < TOKEN_TILES:
-                moments[s] = statistics(s)
-                for ch, c in [divmod(AHEAD * s + i, PASSES) for i in range(AHEAD)]:
-                    grouped[(ch, c)] = regroup(ch, c)
-                    load_wq(ch + AHEAD, c)
-            if 0 <= s - 1 < TOKEN_TILES:
-                flipped_banks[s - 1] = normalise_and_transpose(s - 1, moments[s - 1][0], moments[s - 1][1])
-            if 0 <= s - 2:
-                scale_and_quantise(s - 2, flipped_banks[s - 2])
+
+        def regroup_and_reload(ch, c):
+            grouped[(ch, c)] = regroup(ch, c)
+            if ch + LOADED < Q_CHUNKS:
+                load_wq(ch + LOADED, c)
+
+        for ch in range(AHEAD):
+            for c in range(PASSES):
+                regroup_and_reload(ch, c)
         nc.sync.dma_start(out=kv_raw[:, :, 0, :], in_=wk.rearrange("(g p) n -> p g n", p=P))
         nc.sync.dma_start(out=kv_raw[:, :, 1, :], in_=wv.rearrange("(g p) n -> p g n", p=P))
 
         sums = {}
         for ch in range(CHUNKS + 1):
             if ch < CHUNKS:
-                for c in range(PASSES):
-                    quantise(ch, c, grouped[(ch, c)])
-                    if ch + AHEAD < CHUNKS:
-                        grouped[(ch + AHEAD, c)] = regroup(ch + AHEAD, c)
-            if ch < Q_CHUNKS:
-                for t in range(TOKEN_TILES):
-                    sums[(ch, t)] = psum.tile([P, BANK], F32, tag="bank", name="q_sums")
-                    project(ch, t, sums[(ch, t)][:])
-            if ch == KV:
-                for first in range(0, TOKEN_TILES, 2):
-                    sums[(ch, first)] = psum.tile([P, 2, KV_WIDTH], F32, tag="bank", name="kv_sums")
-                    for u in range(2):
-                        project(ch, first + u, sums[(ch, first)][:, u, :])
-            if 1 <= ch <= Q_CHUNKS:
-                for t in range(TOKEN_TILES):
-                    finish_q(ch - 1, t, sums[(ch - 1, t)])
-            if ch == CHUNKS:
-                for first in range(0, TOKEN_TILES, 2):
-                    finish_kv(first, sums[(KV, first)])
+                sums[ch] = [
+                    psum.tile([P, widths[ch]], F32, tag="bank", name="sums") for t in range(TOKEN_TILES)
+                ]
+            for i in range(PASSES):
+                if ch < CHUNKS:
+                    quantise(ch, i, grouped[(ch, i)])
+                    project(ch, i, sums[ch])
+                if ch + AHEAD < CHUNKS:
+                    regroup_and_reload(ch + AHEAD, i)
+                if 1 <= ch <= Q_CHUNKS:
+                    finish_q(ch - 1, i, sums[ch - 1][i])
+                if ch == CHUNKS:
+                    finish_kv(i, sums[KV][i])

@@ -97,21 +97,20 @@ def tile_attention_pa_kernel(tc, x, gamma, wq, wk, wv, sin, cos, out_0, out_1, o
             out=mean_weights[:], in0=ident_bf16[:], scalar1=1.0 / D_MODEL, scalar2=None, op0=ALU.mult
         )
 
-        def rotary_tables(scale, label):
-            by_even = keep.tile([P, TOKEN_TILES, 2, PAIRS], F32, name="by_even_" + label)
-            by_odd = keep.tile([P, TOKEN_TILES, 2, PAIRS], F32, name="by_odd_" + label)
-            cos_pairs = cos_raw[:].rearrange("p t (i e) -> p t i e", e=2)
-            sin_pairs = sin_raw[:].rearrange("p t (i e) -> p t i e", e=2)
-            for table, r, source, factor in (
-                (by_even, 0, cos_pairs[:, :, :, 0], scale),
-                (by_even, 1, sin_pairs[:, :, :, 1], scale),
-                (by_odd, 0, sin_pairs[:, :, :, 0], -scale),
-                (by_odd, 1, cos_pairs[:, :, :, 1], scale),
-            ):
+        def rotary_tables():
+            k_factor = keep.tile([P, TOKEN_TILES, 2, D_HEAD], F32)
+            entries = k_factor[:].rearrange("p t s (i r) -> p t s i r", r=2)
+            cos_pairs = cos_raw[:].rearrange("p t (i r) -> p t i r", r=2)
+            sin_pairs = sin_raw[:].rearrange("p t (i r) -> p t i r", r=2)
+            for s, r, source, sign in ((0, 0, cos_pairs, 1.0), (0, 1, sin_pairs, 1.0), (1, 0, sin_pairs, -1.0), (1, 1, cos_pairs, 1.0)):
                 nc.gpsimd.tensor_scalar(
-                    out=table[:, :, r, :], in0=source, scalar1=factor, scalar2=0.0, op0=ALU.mult, op1=ALU.add
+                    out=entries[:, :, s, :, r], in0=source[:, :, :, r], scalar1=sign, scalar2=0.0, op0=ALU.mult, op1=ALU.add
                 )
-            return by_even, by_odd
+            q_factor = keep.tile([P, TOKEN_TILES, 2, D_HEAD], F32)
+            nc.gpsimd.tensor_scalar(
+                out=q_factor[:], in0=k_factor[:], scalar1=D_HEAD**-0.5, scalar2=0.0, op0=ALU.mult, op1=ALU.add
+            )
+            return q_factor, k_factor
 
         x_codes = keep.tile([P, TOKEN_TILES, PASSES, P], U32, align_bytes=64)
         x_scales = keep.tile([P, TOKEN_TILES, PASSES, P], U8, align_bytes=64)
@@ -225,45 +224,26 @@ def tile_attention_pa_kernel(tc, x, gamma, wq, wk, wv, sin, cos, out_0, out_1, o
                     stop=(c == PASSES - 1),
                 )
 
-        def rotate(result, sums, by_even, by_odd, n):
-            pairs = sums.rearrange("p n (i e) -> p e n i", e=2)
-            from_even = rotary.tile([P, 2, n, PAIRS], F32, tag="from_even")
+        def rotate(result, sums, factor, n):
+            shape = [P, 2, n, PAIRS, 2]
+            products = rotary.tile([P, 2, n, D_HEAD], F32, tag="products")
             nc.vector.tensor_tensor(
-                out=from_even[:], in0=pairs[:, 0:1].to_broadcast([P, 2, n, PAIRS]), in1=by_even, op=ALU.mult
+                out=products[:].rearrange("p s n (i r) -> p s n i r", r=2),
+                in0=sums.rearrange("p n (i s) -> p s n i", s=2).unsqueeze(4).to_broadcast(shape),
+                in1=factor.rearrange("p s (i r) -> p s i r", r=2).unsqueeze(2).to_broadcast(shape),
+                op=ALU.mult,
             )
-            from_odd = rotary.tile([P, 2, n, PAIRS], F32, tag="from_odd")
-            nc.vector.tensor_tensor(
-                out=from_odd[:], in0=pairs[:, 1:2].to_broadcast([P, 2, n, PAIRS]), in1=by_odd, op=ALU.mult
-            )
-            nc.gpsimd.tensor_tensor(
-                out=result.rearrange("p n (i r) -> p n i r", r=2),
-                in0=from_even[:].rearrange("p r n i -> p n i r"),
-                in1=from_odd[:].rearrange("p r n i -> p n i r"),
-                op=ALU.add,
-            )
+            nc.gpsimd.tensor_tensor(out=result, in0=products[:, 0], in1=products[:, 1], op=ALU.add)
 
         def finish_q(ch, t, sums):
-            q_rot = rotary.tile([P, HEADS_PER_CHUNK, D_HEAD], F32, tag="rotated")
-            shape = [P, 2, HEADS_PER_CHUNK, PAIRS]
-            rotate(
-                q_rot[:],
-                sums[:].rearrange("p (n d) -> p n d", d=D_HEAD),
-                q_by_even[:, t].unsqueeze(2).to_broadcast(shape),
-                q_by_odd[:, t].unsqueeze(2).to_broadcast(shape),
-                HEADS_PER_CHUNK,
-            )
+            q_rot = rotary.tile([P, HEADS_PER_CHUNK, D_HEAD], F32, tag="q_rot")
+            rotate(q_rot[:], sums[:].rearrange("p (n d) -> p n d", d=D_HEAD), q_factor[:, t], HEADS_PER_CHUNK)
             heads = out_0[0, ch * HEADS_PER_CHUNK : (ch + 1) * HEADS_PER_CHUNK, t * P : (t + 1) * P, :]
             nc.sync.dma_start(out=heads.rearrange("h m d -> m h d"), in_=q_rot[:])
 
         def finish_kv(t, sums):
             k_rot = rotary.tile([P, 1, D_HEAD], F32, tag="k_rot")
-            rotate(
-                k_rot[:],
-                sums[:, 0:D_HEAD].unsqueeze(1),
-                k_by_even[:, t].unsqueeze(2),
-                k_by_odd[:, t].unsqueeze(2),
-                1,
-            )
+            rotate(k_rot[:], sums[:, 0:D_HEAD].unsqueeze(1), k_factor[:, t], 1)
             v_copy = rotary.tile([P, D_HEAD], F32, tag="v_copy")
             nc.scalar.copy(out=v_copy[:], in_=sums[:, D_HEAD:KV_WIDTH])
             token_rows = slice(t * P, (t + 1) * P)
@@ -286,8 +266,7 @@ def tile_attention_pa_kernel(tc, x, gamma, wq, wk, wv, sin, cos, out_0, out_1, o
                 stats[s + 1] = moments(s + 1, folds[s + 1])
             if s >= 1:
                 scale_and_quantise(s - 1, flipped_banks[s - 1])
-        q_by_even, q_by_odd = rotary_tables(D_HEAD**-0.5, "q")
-        k_by_even, k_by_odd = rotary_tables(1.0, "k")
+        q_factor, k_factor = rotary_tables()
 
         grouped = {}
 

@@ -35,7 +35,7 @@ AHEAD = 1
 REGROUPED = 2
 LOADED = 3
 RUN = 4
-VECTOR_EVERY = 8
+VECTOR_UNIT = (1, 3)
 NORM_PASSES = 2
 
 FLOPS = 2 * TOKENS * D_MODEL * (HEADS * D_HEAD + KV_WIDTH)
@@ -199,7 +199,7 @@ def tile_attention_pa_kernel(tc, x, gamma, wq, wk, wv, sin, cos, out_0, out_1, o
             grouped = regrouped.tile([P, widths[ch], PACK], BF16, tag="grouped", align_bytes=64)
             target = grouped[:].rearrange("p (a i) j -> p a j i", i=RUN)
             source = weight_rows(ch, c).rearrange("p j (a i) -> p a j i", i=RUN)
-            if (ch * PASSES + c) % VECTOR_EVERY == VECTOR_EVERY - 1:
+            if (ch, c) == VECTOR_UNIT:
                 nc.vector.tensor_copy(out=target, in_=source)
             else:
                 nc.scalar.copy(out=target, in_=source)
@@ -224,7 +224,7 @@ def tile_attention_pa_kernel(tc, x, gamma, wq, wk, wv, sin, cos, out_0, out_1, o
                     stop=(c == PASSES - 1),
                 )
 
-        def rotate(result, sums, factor, n):
+        def rotate(result, sums, factor, n, adder):
             shape = [P, 2, n, PAIRS, 2]
             products = rotary.tile([P, 2, n, D_HEAD], F32, tag="products")
             nc.vector.tensor_tensor(
@@ -233,22 +233,20 @@ def tile_attention_pa_kernel(tc, x, gamma, wq, wk, wv, sin, cos, out_0, out_1, o
                 in1=factor.rearrange("p s (i r) -> p s i r", r=2).unsqueeze(2).to_broadcast(shape),
                 op=ALU.mult,
             )
-            nc.gpsimd.tensor_tensor(out=result, in0=products[:, 0], in1=products[:, 1], op=ALU.add)
+            adder.tensor_tensor(out=result, in0=products[:, 0], in1=products[:, 1], op=ALU.add)
 
         def finish_q(ch, t, sums):
             q_rot = rotary.tile([P, HEADS_PER_CHUNK, D_HEAD], F32, tag="q_rot")
-            rotate(q_rot[:], sums[:].rearrange("p (n d) -> p n d", d=D_HEAD), q_factor[:, t], HEADS_PER_CHUNK)
+            rotate(q_rot[:], sums[:].rearrange("p (n d) -> p n d", d=D_HEAD), q_factor[:, t], HEADS_PER_CHUNK, nc.gpsimd)
             heads = out_0[0, ch * HEADS_PER_CHUNK : (ch + 1) * HEADS_PER_CHUNK, t * P : (t + 1) * P, :]
             nc.sync.dma_start(out=heads.rearrange("h m d -> m h d"), in_=q_rot[:])
 
+        k_rot = keep.tile([P, TOKEN_TILES, D_HEAD], F32)
+        v_copy = keep.tile([P, TOKEN_TILES, D_HEAD], F32)
+
         def finish_kv(t, sums):
-            k_rot = rotary.tile([P, 1, D_HEAD], F32, tag="k_rot")
-            rotate(k_rot[:], sums[:, 0:D_HEAD].unsqueeze(1), k_factor[:, t], 1)
-            v_copy = rotary.tile([P, D_HEAD], F32, tag="v_copy")
-            nc.scalar.copy(out=v_copy[:], in_=sums[:, D_HEAD:KV_WIDTH])
-            token_rows = slice(t * P, (t + 1) * P)
-            nc.sync.dma_start(out=out_1[0, token_rows, :], in_=k_rot[:, 0, :])
-            nc.sync.dma_start(out=out_2[0, token_rows, :], in_=v_copy[:])
+            rotate(k_rot[:, t : t + 1], sums[:, 0:D_HEAD].unsqueeze(1), k_factor[:, t], 1, nc.vector)
+            nc.scalar.copy(out=v_copy[:, t], in_=sums[:, D_HEAD:KV_WIDTH])
 
         folds = {0: fold(0)}
         gamma_ps = psum.tile([P, P], BF16, tag="bank")
@@ -297,3 +295,5 @@ def tile_attention_pa_kernel(tc, x, gamma, wq, wk, wv, sin, cos, out_0, out_1, o
                     finish_q(ch - 1, i, sums[ch - 1][i])
                 if ch == CHUNKS:
                     finish_kv(i, sums[KV][i])
+        nc.sync.dma_start(out=out_2[0].rearrange("(t m) d -> m t d", m=P), in_=v_copy[:])
+        nc.sync.dma_start(out=out_1[0].rearrange("(t m) d -> m t d", m=P), in_=k_rot[:])

@@ -35,7 +35,7 @@ AHEAD = 1
 REGROUPED = 2
 LOADED = 3
 RUN = 4
-VECTOR_UNIT = (1, 3)
+VECTOR_EVERY = 8
 NORM_PASSES = 2
 
 FLOPS = 2 * TOKENS * D_MODEL * (HEADS * D_HEAD + KV_WIDTH)
@@ -199,7 +199,7 @@ def tile_attention_pa_kernel(tc, x, gamma, wq, wk, wv, sin, cos, out_0, out_1, o
             grouped = regrouped.tile([P, widths[ch], PACK], BF16, tag="grouped", align_bytes=64)
             target = grouped[:].rearrange("p (a i) j -> p a j i", i=RUN)
             source = weight_rows(ch, c).rearrange("p j (a i) -> p a j i", i=RUN)
-            if (ch, c) == VECTOR_UNIT:
+            if (ch * PASSES + c) % VECTOR_EVERY == VECTOR_EVERY - 1:
                 nc.vector.tensor_copy(out=target, in_=source)
             else:
                 nc.scalar.copy(out=target, in_=source)
@@ -224,7 +224,7 @@ def tile_attention_pa_kernel(tc, x, gamma, wq, wk, wv, sin, cos, out_0, out_1, o
                     stop=(c == PASSES - 1),
                 )
 
-        def rotate(result, sums, factor, n, adder):
+        def rotate(result, sums, factor, n):
             shape = [P, 2, n, PAIRS, 2]
             products = rotary.tile([P, 2, n, D_HEAD], F32, tag="products")
             nc.vector.tensor_tensor(
@@ -233,11 +233,11 @@ def tile_attention_pa_kernel(tc, x, gamma, wq, wk, wv, sin, cos, out_0, out_1, o
                 in1=factor.rearrange("p s (i r) -> p s i r", r=2).unsqueeze(2).to_broadcast(shape),
                 op=ALU.mult,
             )
-            adder.tensor_tensor(out=result, in0=products[:, 0], in1=products[:, 1], op=ALU.add)
+            nc.gpsimd.tensor_tensor(out=result, in0=products[:, 0], in1=products[:, 1], op=ALU.add)
 
         def finish_q(ch, t, sums):
             q_rot = rotary.tile([P, HEADS_PER_CHUNK, D_HEAD], F32, tag="q_rot")
-            rotate(q_rot[:], sums[:].rearrange("p (n d) -> p n d", d=D_HEAD), q_factor[:, t], HEADS_PER_CHUNK, nc.gpsimd)
+            rotate(q_rot[:], sums[:].rearrange("p (n d) -> p n d", d=D_HEAD), q_factor[:, t], HEADS_PER_CHUNK)
             heads = out_0[0, ch * HEADS_PER_CHUNK : (ch + 1) * HEADS_PER_CHUNK, t * P : (t + 1) * P, :]
             nc.sync.dma_start(out=heads.rearrange("h m d -> m h d"), in_=q_rot[:])
 
@@ -245,7 +245,7 @@ def tile_attention_pa_kernel(tc, x, gamma, wq, wk, wv, sin, cos, out_0, out_1, o
         v_copy = keep.tile([P, TOKEN_TILES, D_HEAD], F32)
 
         def finish_kv(t, sums):
-            rotate(k_rot[:, t : t + 1], sums[:, 0:D_HEAD].unsqueeze(1), k_factor[:, t], 1, nc.vector)
+            rotate(k_rot[:, t : t + 1], sums[:, 0:D_HEAD].unsqueeze(1), k_factor[:, t], 1)
             nc.scalar.copy(out=v_copy[:, t], in_=sums[:, D_HEAD:KV_WIDTH])
 
         folds = {0: fold(0)}

from contextlib import ExitStack

import concourse.mybir as mybir
from concourse.masks import make_identity

F32 = mybir.dt.float32
BF16 = mybir.dt.bfloat16
U32 = mybir.dt.uint32
U8 = mybir.dt.uint8
FP8X4 = mybir.dt.float8_e4m3fn_x4
ALU = mybir.AluOpType
ACT = mybir.ActivationFunctionType
AXIS = mybir.AxisListType

P = 128
PACK = 4
K_PASS = P * PACK
TOKENS = 512
D_MODEL = 2048
HEADS = 16
D_HEAD = 128
EPS = 1e-5

TOKEN_TILES = TOKENS // P
PASSES = D_MODEL // K_PASS
ROW_GROUPS = D_MODEL // P
PAIRS = D_HEAD // 2
BANK = 512
Q_CHUNKS = HEADS * D_HEAD // BANK
HEADS_PER_CHUNK = BANK // D_HEAD
KV = Q_CHUNKS
CHUNKS = Q_CHUNKS + 1
KV_WIDTH = 2 * D_HEAD
AHEAD = 1
REGROUPED = 2
LOADED = 3
RUN = 4
VECTOR_EVERY = 8
NORM_PASSES = 2

FLOPS = 2 * TOKENS * D_MODEL * (HEADS * D_HEAD + KV_WIDTH)


def tile_attention_pa_kernel(tc, x, gamma, wq, wk, wv, sin, cos, out_0, out_1, out_2):
    nc = tc.nc
    with ExitStack() as ctx:
        keep = ctx.enter_context(tc.tile_pool(name="keep", bufs=1))
        small = ctx.enter_context(tc.tile_pool(name="small", bufs=4))
        rows = ctx.enter_context(tc.tile_pool(name="rows", bufs=2))
        loaded = ctx.enter_context(tc.tile_pool(name="loaded", bufs=LOADED * PASSES))
        regrouped = ctx.enter_context(tc.tile_pool(name="regrouped", bufs=REGROUPED * PASSES))
        rotary = ctx.enter_context(tc.tile_pool(name="rotary", bufs=4))
        psum = ctx.enter_context(tc.psum_pool(name="psum", bufs=8))
        ctx.enter_context(tc.manual_schedule())

        x_tiles = x.rearrange("b (t p) k -> (b t) p k", p=P)
        x_raw = {}

        def load_x(t):
            x_raw[t] = keep.tile([P, D_MODEL], BF16, name="x_raw%d" % t)
            nc.sync.dma_start(out=x_raw[t][:], in_=x_tiles[t])

        wq_passes = wq.rearrange("(c j p) n -> c p j n", j=PACK, p=P)
        wq_raw = {}

        def load_wq(ch, c):
            wq_raw[(ch, c)] = loaded.tile([P, PACK, BANK], BF16, name="wq_raw")
            nc.sync.dma_start(out=wq_raw[(ch, c)][:], in_=wq_passes[c][:, :, ch * BANK : (ch + 1) * BANK])

        gamma_rows = keep.tile([P, P], BF16)
        nc.vector.memset(gamma_rows[:], 0.0)
        nc.scalar.dma_start(out=gamma_rows[0:ROW_GROUPS, :], in_=gamma.rearrange("(g p) -> g p", p=P))
        for t in range(TOKEN_TILES):
            load_x(t)
        for c in range(PASSES):
            load_wq(0, c)
        cos_raw = keep.tile([P, TOKEN_TILES, D_HEAD], BF16)
        nc.sync.dma_start(out=cos_raw[:], in_=cos.rearrange("(t p) d -> p t d", p=P))
        sin_raw = keep.tile([P, TOKEN_TILES, D_HEAD], BF16)
        nc.sync.dma_start(out=sin_raw[:], in_=sin.rearrange("(t p) d -> p t d", p=P))
        for ch in range(1, LOADED):
            for c in range(PASSES):
                load_wq(ch, c)

        kv_raw = keep.tile([P, ROW_GROUPS, 2, D_HEAD], BF16)

        ident_f32 = keep.tile([P, P], F32)
        make_identity(nc, ident_f32[:])
        ident_bf16 = keep.tile([P, P], BF16)
        make_identity(nc, ident_bf16[:])
        one = keep.tile([P, 1], F32)
        nc.vector.memset(one[:], 1.0)
        table_warm = keep.tile([P, 1], F32)
        nc.scalar.activation(out=table_warm[:], in_=one[:], func=ACT.Sqrt)
        mean_weights = keep.tile([P, P], BF16)
        nc.vector.tensor_scalar(
            out=mean_weights[:], in0=ident_bf16[:], scalar1=1.0 / D_MODEL, scalar2=None, op0=ALU.mult
        )

        def rotary_tables():
            k_factor = keep.tile([P, TOKEN_TILES, 2, D_HEAD], F32)
            entries = k_factor[:].rearrange("p t s (i r) -> p t s i r", r=2)
            cos_pairs = cos_raw[:].rearrange("p t (i r) -> p t i r", r=2)
            sin_pairs = sin_raw[:].rearrange("p t (i r) -> p t i r", r=2)
            for s, r, source, sign in ((0, 0, cos_pairs, 1.0), (0, 1, sin_pairs, 1.0), (1, 0, sin_pairs, -1.0), (1, 1, cos_pairs, 1.0)):
                nc.gpsimd.tensor_scalar(
                    out=entries[:, :, s, :, r], in0=source[:, :, :, r], scalar1=sign, scalar2=0.0, op0=ALU.mult, op1=ALU.add
                )
            q_factor = keep.tile([P, TOKEN_TILES, 2, D_HEAD], F32)
            nc.gpsimd.tensor_scalar(
                out=q_factor[:], in0=k_factor[:], scalar1=D_HEAD**-0.5, scalar2=0.0, op0=ALU.mult, op1=ALU.add
            )
            return q_factor, k_factor

        x_codes = keep.tile([P, TOKEN_TILES, PASSES, P], U32, align_bytes=64)
        x_scales = keep.tile([P, TOKEN_TILES, PASSES, P], U8, align_bytes=64)
        widths = [BANK] * Q_CHUNKS + [KV_WIDTH]
        w_codes = [
            keep.tile([P, PASSES, widths[ch]], U32, align_bytes=64, name="w_codes%d" % ch) for ch in range(CHUNKS)
        ]
        w_scales = [
            keep.tile([P, PASSES, widths[ch]], U8, align_bytes=64, name="w_scales%d" % ch) for ch in range(CHUNKS)
        ]

        def fold(t):
            folded = psum.tile([P, P], F32, tag="bank")
            for g in range(ROW_GROUPS):
                nc.tensor.matmul(
                    folded[:],
                    lhsT=mean_weights[:],
                    rhs=x_raw[t][:, g * P : (g + 1) * P],
                    start=(g == 0),
                    stop=(g == ROW_GROUPS - 1),
                )
            return folded

        def moments(t, folded):
            squares = keep.tile([P, D_MODEL], BF16, name="squares")
            sum_sq = small.tile([P, 1], F32)
            nc.scalar.activation(out=squares[:], in_=x_raw[t][:], func=ACT.Square, accum_out=sum_sq[:])
            mean = small.tile([P, 1], F32)
            nc.vector.tensor_reduce(out=mean[:], in_=folded[:], axis=AXIS.X, op=ALU.add)
            minus_mean = small.tile([P, 1], F32)
            nc.vector.tensor_scalar(out=minus_mean[:], in0=mean[:], scalar1=-1.0, scalar2=None, op0=ALU.mult)
            shift = small.tile([P, 1], F32)
            nc.vector.tensor_scalar(
                out=shift[:], in0=mean[:], scalar1=minus_mean[:, 0:1], scalar2=EPS, op0=ALU.mult, op1=ALU.add
            )
            std = small.tile([P, 1], F32)
            nc.scalar.activation(
                out=std[:], in_=sum_sq[:], func=ACT.Sqrt, bias=shift[:, 0:1], scale=1.0 / D_MODEL
            )
            return minus_mean, std

        def normalise_and_transpose(t, minus_mean, std):
            rstd = small.tile([P, 1], F32)
            nc.vector.reciprocal(out=rstd[:], in_=std[:])
            centred = rows.tile([P, D_MODEL], F32)
            banks = []
            for c in range(PASSES):
                if c % NORM_PASSES == 0:
                    features = slice(c * K_PASS, (c + NORM_PASSES) * K_PASS)
                    nc.gpsimd.tensor_scalar(
                        out=centred[:, features],
                        in0=x_raw[t][:, features],
                        scalar1=minus_mean[:, 0:1],
                        scalar2=rstd[:, 0:1],
                        op0=ALU.add,
                        op1=ALU.mult,
                    )
                flipped = psum.tile([P, PACK, P], F32, tag="bank", name="flipped")
                for j in range(PACK):
                    g = c * PACK + j
                    nc.tensor.transpose(flipped[:, j, :], centred[:, g * P : (g + 1) * P], ident_f32[:])
                banks.append(flipped)
            return banks

        def scale_and_quantise(t, banks):
            xn = rows.tile([P, PASSES, P, PACK], BF16, align_bytes=64)
            for c in range(PASSES):
                nc.vector.tensor_tensor(
                    out=xn[:, c, :, :],
                    in0=banks[c][:].rearrange("p j m -> p m j"),
                    in1=gamma_col[:, c * PACK : (c + 1) * PACK].unsqueeze(1).to_broadcast([P, P, PACK]),
                    op=ALU.mult,
                )
            nc.vector.quantize_mx(
                out=x_codes[:, t].rearrange("p c m -> p (c m)").bitcast(FP8X4),
                scales=x_scales[:, t].rearrange("p c m -> p (c m)"),
                in_=xn[:].rearrange("p c m j -> p (c m j)"),
            )

        def weight_rows(ch, c):
            if ch == KV:
                return kv_raw[:, c * PACK : (c + 1) * PACK, :, :].rearrange("p j s n -> p j (s n)")
            return wq_raw[(ch, c)][:]

        def regroup(ch, c):
            grouped = regrouped.tile([P, widths[ch], PACK], BF16, tag="grouped", align_bytes=64)
            target = grouped[:].rearrange("p (a i) j -> p a j i", i=RUN)
            source = weight_rows(ch, c).rearrange("p j (a i) -> p a j i", i=RUN)
            if (ch * PASSES + c) % VECTOR_EVERY == VECTOR_EVERY - 1:
                nc.vector.tensor_copy(out=target, in_=source)
            else:
                nc.scalar.copy(out=target, in_=source)
            return grouped

        def quantise(ch, c, grouped):
            nc.vector.quantize_mx(
                out=w_codes[ch][:, c, :].bitcast(FP8X4),
                scales=w_scales[ch][:, c, :],
                in_=grouped[:].rearrange("p n j -> p (n j)"),
            )

        def project(ch, c, sums):
            for t in range(TOKEN_TILES):
                nc.tensor.matmul_mx(
                    out=sums[t][:],
                    lhsT=x_codes[:, t, c, :].bitcast(FP8X4),
                    lhsT_scale=x_scales[:, t, c, :],
                    rhs=w_codes[ch][:, c, :].bitcast(FP8X4),
                    rhs_scale=w_scales[ch][:, c, :],
                    start=(c == 0),
                    stop=(c == PASSES - 1),
                )

        def rotate(result, sums, factor, n):
            shape = [P, 2, n, PAIRS, 2]
            products = rotary.tile([P, 2, n, D_HEAD], F32, tag="products")
            nc.vector.tensor_tensor(
                out=products[:].rearrange("p s n (i r) -> p s n i r", r=2),
                in0=sums.rearrange("p n (i s) -> p s n i", s=2).unsqueeze(4).to_broadcast(shape),
                in1=factor.rearrange("p s (i r) -> p s i r", r=2).unsqueeze(2).to_broadcast(shape),
                op=ALU.mult,
            )
            nc.gpsimd.tensor_tensor(out=result, in0=products[:, 0], in1=products[:, 1], op=ALU.add)

        def finish_q(ch, t, sums):
            q_rot = rotary.tile([P, HEADS_PER_CHUNK, D_HEAD], F32, tag="q_rot")
            rotate(q_rot[:], sums[:].rearrange("p (n d) -> p n d", d=D_HEAD), q_factor[:, t], HEADS_PER_CHUNK)
            heads = out_0[0, ch * HEADS_PER_CHUNK : (ch + 1) * HEADS_PER_CHUNK, t * P : (t + 1) * P, :]
            nc.sync.dma_start(out=heads.rearrange("h m d -> m h d"), in_=q_rot[:])

        k_rot = keep.tile([P, TOKEN_TILES, D_HEAD], F32)
        v_copy = keep.tile([P, TOKEN_TILES, D_HEAD], F32)

        def finish_kv(t, sums):
            rotate(k_rot[:, t : t + 1], sums[:, 0:D_HEAD].unsqueeze(1), k_factor[:, t], 1)
            nc.scalar.copy(out=v_copy[:, t], in_=sums[:, D_HEAD:KV_WIDTH])

        folds = {0: fold(0)}
        gamma_ps = psum.tile([P, P], BF16, tag="bank")
        nc.tensor.transpose(gamma_ps[:], gamma_rows[:], ident_bf16[:])
        gamma_col = keep.tile([P, ROW_GROUPS], F32)
        nc.vector.tensor_copy(out=gamma_col[:], in_=gamma_ps[:, 0:ROW_GROUPS])
        for t in range(1, TOKEN_TILES):
            folds[t] = fold(t)
        stats = {0: moments(0, folds[0])}
        flipped_banks = {}
        for s in range(TOKEN_TILES + 1):
            if s < TOKEN_TILES:
                flipped_banks[s] = normalise_and_transpose(s, stats[s][0], stats[s][1])
            if s + 1 < TOKEN_TILES:
                stats[s + 1] = moments(s + 1, folds[s + 1])
            if s >= 1:
                scale_and_quantise(s - 1, flipped_banks[s - 1])
        q_factor, k_factor = rotary_tables()

        grouped = {}

        def regroup_and_reload(ch, c):
            grouped[(ch, c)] = regroup(ch, c)
            if ch + LOADED < Q_CHUNKS:
                load_wq(ch + LOADED, c)

        for ch in range(AHEAD):
            for c in range(PASSES):
                regroup_and_reload(ch, c)
        nc.sync.dma_start(out=kv_raw[:, :, 0, :], in_=wk.rearrange("(g p) n -> p g n", p=P))
        nc.sync.dma_start(out=kv_raw[:, :, 1, :], in_=wv.rearrange("(g p) n -> p g n", p=P))

        sums = {}
        for ch in range(CHUNKS + 1):
            if ch < CHUNKS:
                sums[ch] = [
                    psum.tile([P, widths[ch]], F32, tag="bank", name="sums") for t in range(TOKEN_TILES)
                ]
            for i in range(PASSES):
                if ch < CHUNKS:
                    quantise(ch, i, grouped[(ch, i)])
                    project(ch, i, sums[ch])
                if ch + AHEAD < CHUNKS:
                    regroup_and_reload(ch + AHEAD, i)
                if 1 <= ch <= Q_CHUNKS:
                    finish_q(ch - 1, i, sums[ch - 1][i])
                if ch == CHUNKS:
                    finish_kv(i, sums[KV][i])
        nc.sync.dma_start(out=out_2[0].rearrange("(t m) d -> m t d", m=P), in_=v_copy[:])
        nc.sync.dma_start(out=out_1[0].rearrange("(t m) d -> m t d", m=P), in_=k_rot[:])
